import numpy as np
import ml_dtypes


def mxq(x, axis, fmt="e4m3"):
    dtype, down = {"e4m3": (ml_dtypes.float8_e4m3fn, 7), "e5m2": (ml_dtypes.float8_e5m2, 14)}[fmt]
    v = np.moveaxis(np.asarray(x, np.float32).astype(ml_dtypes.bfloat16).astype(np.float64), axis, -1)
    blocks = v.reshape(v.shape[:-1] + (-1, 32))
    amax = np.abs(blocks).max(-1, keepdims=True)
    byte = np.maximum(np.where(amax > 0, np.frexp(amax)[1] - 1 + 127, 0) - down, 1)
    scale = np.exp2(byte - 127.0)
    codes = (blocks / scale).astype(np.float32).astype(dtype).astype(np.float64)
    return np.moveaxis((codes * scale).reshape(v.shape), -1, axis)


WIDE = False


def mx_kscale(k):
    if not WIDE:
        return np.ones(k)
    levels = np.array([10, -10, 5, -5, 0])
    if k % 512:
        return np.exp2(np.random.permutation(np.resize(levels, k // 32))).repeat(32)
    a = np.empty((k // 512, 16))
    for p in range(k // 512):
        a[p, :8] = np.random.permutation(np.resize(levels, 8))
        for g in range(8):
            far = levels[np.abs(levels - a[p, g]) >= 10]
            a[p, g + 8] = far[np.random.randint(len(far))]
    return np.exp2(a.ravel()).repeat(32)


BF16 = ml_dtypes.bfloat16


def bf(x):
    return np.asarray(x, np.float32).astype(BF16)


def f64(x):
    return np.asarray(x).astype(np.float64)


B, S, DIM, QK, EXP, V, G = 1, 1024, 1024, 128, 2048, 1024, 512
W = 2 * QK + 2 * EXP
EPS = 1e-5
ERF_TERMS = 100


def erf(z):
    a = np.minimum(np.abs(z), 6.0)
    a2 = 2.0 * a * a
    term = a.copy()
    tot = a.copy()
    for n in range(1, ERF_TERMS):
        term *= a2
        term /= 2 * n + 1
        tot += term
    return np.sign(z) * 2.0 / np.sqrt(np.pi) * np.exp(-a * a) * tot


def gelu_erf(v):
    return 0.5 * v * (1.0 + erf(v / np.sqrt(2.0)))


def setup_inputs():
    s = mx_kscale(DIM)
    rows = np.exp2(np.random.uniform(-8.0, 1.0, (B, S, 1)))
    off = 0.5 * np.random.standard_normal((B, S, 1))
    gain = np.where(np.arange(W) < 2 * QK, 1.5, 1.0)[:, None]
    return {"x": bf((np.random.standard_normal((B, S, DIM)) + off) * rows),
            "norm_w": bf((1.0 + 0.1 * np.random.standard_normal(DIM)) * s),
            "expand_w": bf(np.random.standard_normal((W, DIM)) * gain / np.sqrt(DIM) / s)}


def reference(x, norm_w, expand_w):
    x = f64(x)
    mu = x.mean(-1, keepdims=True)
    var = ((x - mu) ** 2).mean(-1, keepdims=True)
    h = (x - mu) * (1.0 / np.sqrt(var + EPS)) * f64(norm_w)
    proj = mxq(h, 2, "e4m3") @ mxq(f64(expand_w), 1, "e4m3").T
    q = proj[..., :QK]
    k = proj[..., QK:2 * QK]
    lin = proj[..., 2 * QK:2 * QK + EXP]
    pre = proj[..., 2 * QK + EXP:]
    geglu = lin * gelu_erf(pre)
    return q, k, geglu[..., :EXP - V], geglu[..., EXP - V:]

@@ -1,0 +1,243 @@
+from contextlib import ExitStack
+
+import concourse.mybir as mybir
+from concourse.masks import make_identity
+
+F32 = mybir.dt.float32
+BF16 = mybir.dt.bfloat16
+U32 = mybir.dt.uint32
+U8 = mybir.dt.uint8
+FP8X4 = mybir.dt.float8_e4m3fn_x4
+ACT = mybir.ActivationFunctionType
+ALU = mybir.AluOpType
+
+P = 128
+TOKENS = 1024
+DIM = 1024
+QK = 128
+EXP = 2048
+W_ROWS = 2 * QK + 2 * EXP
+EPS = 1e-5
+
+PACK = 4
+K_PASS = P * PACK
+PASSES = DIM // K_PASS
+TOKEN_TILES = TOKENS // P
+GROUP_ROWS = 2 * P
+GROUPS = W_ROWS // GROUP_ROWS
+N_TILE = 512
+UNITS = EXP // N_TILE
+GROUPS_PER_UNIT = 2 * N_TILE // GROUP_ROWS
+GROUPS_PER_TOKEN_TILE = (GROUPS - 1) // TOKEN_TILES
+BN_CHUNK = 512
+PSUM_BANKS = 8
+AHEAD = 2
+
+FLOPS = 2 * TOKENS * DIM * W_ROWS
+
+
+def tile_latentattentionblock_pa_kernel(tc, x, norm_w, expand_w, q_out, k_out, gl_out, gv_out):
+    nc = tc.nc
+    x_view = x.rearrange("b (p m) k -> p (b m) k", m=TOKEN_TILES)
+    q_view = q_out.rearrange("b (p m) c -> p (b m) c", m=TOKEN_TILES)
+    k_view = k_out.rearrange("b (p m) c -> p (b m) c", m=TOKEN_TILES)
+    g_views = [
+        gl_out.rearrange("b (p m) c -> p (b m) c", m=TOKEN_TILES),
+        gv_out.rearrange("b (p m) c -> p (b m) c", m=TOKEN_TILES),
+    ]
+
+    with ExitStack() as ctx:
+        ctx.enter_context(tc.manual_schedule())
+        const = ctx.enter_context(tc.tile_pool(name="const", bufs=1))
+        x_pool = ctx.enter_context(tc.tile_pool(name="x_pool", bufs=TOKEN_TILES))
+        w_pool = ctx.enter_context(tc.tile_pool(name="w_pool", bufs=8))
+        small = ctx.enter_context(tc.tile_pool(name="small", bufs=4))
+        y_pool = ctx.enter_context(tc.tile_pool(name="y_pool", bufs=AHEAD + 1))
+        h_pool = ctx.enter_context(tc.tile_pool(name="h_pool", bufs=3))
+        wg_pool = ctx.enter_context(tc.tile_pool(name="wg_pool", bufs=GROUPS))
+        out_pool = ctx.enter_context(tc.tile_pool(name="out_pool", bufs=4))
+        psum = ctx.enter_context(tc.psum_pool(name="psum", bufs=PSUM_BANKS))
+
+        h_codes = const.tile([P, TOKEN_TILES, PASSES, P], U32, align_bytes=64)
+        h_scales = const.tile([P, TOKEN_TILES, PASSES, P], U8, align_bytes=64)
+        w_codes = const.tile([P, PASSES, W_ROWS], U32, align_bytes=64)
+        w_scales = const.tile([P, PASSES, W_ROWS], U8, align_bytes=64)
+        qk_sb = const.tile([P, 2, TOKEN_TILES, QK], F32)
+
+        first_lin = 1
+        first_pre = 1 + EXP // GROUP_ROWS
+        group_order = [0]
+        for j in range(UNITS):
+            group_order.extend([first_pre + 2 * j, first_pre + 2 * j + 1, first_lin + 2 * j, first_lin + 2 * j + 1])
+
+        def groups_beside(m):
+            return group_order[GROUPS_PER_TOKEN_TILE * m : GROUPS_PER_TOKEN_TILE * (m + 1)]
+
+        groups_after = group_order[GROUPS_PER_TOKEN_TILE * TOKEN_TILES :]
+
+        nw_bf = const.tile([P, PASSES, PACK], BF16)
+        nc.scalar.dma_start(out=nw_bf[:], in_=norm_w.rearrange("(g p t) -> p g t", g=PASSES, t=PACK))
+        minus_half = const.tile([P, 1], F32)
+        nc.vector.memset(minus_half[:], -0.5)
+        ident = const.tile([P, P], F32)
+        make_identity(nc, ident[:])
+        table_warmer = const.tile([P, 1], F32)
+        nc.scalar.activation(out=table_warmer[:], in_=minus_half[:], func=ACT.Gelu)
+
+        x_raw = {}
+        w_raw = {}
+
+        def load_tokens(m):
+            x_tile = x_pool.tile([P, DIM], BF16)
+            nc.sync.dma_start(out=x_tile[:], in_=x_view[:, m, :])
+            x_raw[m] = x_tile
+
+        def load_weights(w):
+            w_chunk = w_pool.tile([P, 2, DIM], BF16)
+            nc.sync.dma_start(
+                out=w_chunk[:],
+                in_=expand_w[GROUP_ROWS * w : GROUP_ROWS * (w + 1), :].rearrange("(p t) k -> p t k", t=2),
+            )
+            w_raw[w] = w_chunk
+
+        for m in range(AHEAD):
+            load_tokens(m)
+        for m in range(TOKEN_TILES):
+            for w in groups_beside(m):
+                load_weights(w)
+            if m + AHEAD < TOKEN_TILES:
+                load_tokens(m + AHEAD)
+        for w in groups_after:
+            load_weights(w)
+
+        nw_cols = const.tile([P, PASSES * PACK], F32)
+        nc.vector.tensor_copy(out=nw_cols[:], in_=nw_bf[:].rearrange("p g t -> p (g t)"))
+
+        y_tiles = {}
+        h_grouped_tiles = {}
+        w_grouped_tiles = {}
+
+        def normalise(m):
+            stats = small.tile([P, DIM // BN_CHUNK, 6], F32)
+            for c in range(DIM // BN_CHUNK):
+                nc.vector.bn_stats(out=stats[:, c, :], in_=x_raw[m][:, BN_CHUNK * c : BN_CHUNK * (c + 1)])
+            mean_var = small.tile([P, 2], F32)
+            nc.vector.bn_aggr(out=mean_var[:], in_=stats[:].rearrange("p c s -> p (c s)"))
+            var_eps = small.tile([P, 1], F32)
+            nc.gpsimd.tensor_scalar(out=var_eps[:], in0=mean_var[:, 1:2], scalar1=EPS, scalar2=None, op0=ALU.add)
+            rstd = small.tile([P, 1], F32)
+            nc.gpsimd.tensor_tensor(out=rstd[:], in0=var_eps[:], in1=minus_half[:], op=ALU.pow)
+            minus_mean = small.tile([P, 1], F32)
+            nc.gpsimd.tensor_scalar(
+                out=minus_mean[:], in0=mean_var[:, 0:1], scalar1=-1.0, scalar2=0.0, op0=ALU.mult, op1=ALU.add
+            )
+            y = y_pool.tile([P, PACK, DIM // PACK], F32)
+            nc.gpsimd.tensor_scalar(
+                out=y[:],
+                in0=x_raw[m][:].rearrange("p (j t) -> p t j", t=PACK),
+                scalar1=minus_mean[:, 0:1],
+                scalar2=rstd[:, 0:1],
+                op0=ALU.add,
+                op1=ALU.mult,
+            )
+            y_tiles[m] = y
+
+        def transpose_tokens(m):
+            y = y_tiles[m]
+            h_grouped = h_pool.tile([P, PASSES, P, PACK], BF16, align_bytes=64)
+            for g in range(PASSES):
+                yt = psum.tile([P, PACK, P], F32, tag="bank")
+                for t in range(PACK):
+                    nc.tensor.transpose(yt[:, t, :], y[:, t, P * g : P * (g + 1)], ident[:])
+                nc.vector.tensor_tensor(
+                    out=h_grouped[:, g, :, :],
+                    in0=yt[:].rearrange("p t r -> p r t"),
+                    in1=nw_cols[:, PACK * g : PACK * (g + 1)].unsqueeze(1).to_broadcast([P, P, PACK]),
+                    op=ALU.mult,
+                )
+            h_grouped_tiles[m] = h_grouped
+
+        def quantise_tokens(m):
+            nc.vector.quantize_mx(
+                out=h_codes[:, m, :, :].rearrange("p g r -> p (g r)").bitcast(FP8X4),
+                scales=h_scales[:, m, :, :].rearrange("p g r -> p (g r)"),
+                in_=h_grouped_tiles[m][:].rearrange("p g r t -> p (g r t)"),
+            )
+
+        def transpose_weights(w):
+            words = w_raw[w][:].bitcast(F32)
+            w_grouped = wg_pool.tile([P, PASSES, GROUP_ROWS * PACK], BF16, align_bytes=64)
+            for g in range(PASSES):
+                wt = psum.tile([P, 2, 2, P], F32, tag="bank")
+                for t in range(2):
+                    for u in range(2):
+                        nc.tensor.transpose(wt[:, t, u, :], words[:, t, 2 * P * g + u : 2 * P * (g + 1) : 2], ident[:])
+                nc.scalar.copy(
+                    out=w_grouped[:, g, :].bitcast(F32).rearrange("p (r t u) -> p r t u", t=2, u=2),
+                    in_=wt[:].rearrange("p t u r -> p r t u"),
+                )
+            w_grouped_tiles[w] = w_grouped
+
+        def quantise_weights(w):
+            cols = slice(GROUP_ROWS * w, GROUP_ROWS * (w + 1))
+            for g in range(PASSES):
+                nc.vector.quantize_mx(
+                    out=w_codes[:, g, cols].bitcast(FP8X4),
+                    scales=w_scales[:, g, cols],
+                    in_=w_grouped_tiles[w][:, g, :],
+                )
+
+        def project(acc, m, first, width):
+            for g in range(PASSES):
+                nc.tensor.matmul_mx(
+                    out=acc,
+                    lhsT=h_codes[:, m, g, :].bitcast(FP8X4),
+                    lhsT_scale=h_scales[:, m, g, :],
+                    rhs=w_codes[:, g, first : first + width].bitcast(FP8X4),
+                    rhs_scale=w_scales[:, g, first : first + width],
+                    start=(g == 0),
+                    stop=(g == PASSES - 1),
+                )
+
+        def q_and_k(m):
+            qk = psum.tile([P, 2, QK], F32, tag="bank")
+            project(qk[:].rearrange("p a c -> p (a c)"), m, 0, 2 * QK)
+            nc.scalar.copy(out=qk_sb[:, :, m, :], in_=qk[:])
+
+        def geglu(j, m):
+            pre = psum.tile([P, N_TILE], F32, tag="bank")
+            project(pre[:], m, 2 * QK + EXP + N_TILE * j, N_TILE)
+            lin = psum.tile([P, N_TILE], F32, tag="bank")
+            project(lin[:], m, 2 * QK + N_TILE * j, N_TILE)
+            gelu = out_pool.tile([P, N_TILE], F32)
+            nc.scalar.activation(out=gelu[:], in_=pre[:], func=ACT.Gelu)
+            prod = out_pool.tile([P, N_TILE], F32)
+            nc.vector.tensor_tensor(out=prod[:], in0=lin[:], in1=gelu[:], op=ALU.mult)
+            first = N_TILE * (j % 2)
+            nc.sync.dma_start(out=g_views[j // 2][:, m, first : first + N_TILE], in_=prod[:])
+
+        for m in range(AHEAD):
+            normalise(m)
+        for m in range(TOKEN_TILES):
+            if m + AHEAD < TOKEN_TILES:
+                normalise(m + AHEAD)
+            transpose_tokens(m)
+            if m >= 1:
+                quantise_tokens(m - 1)
+            for w in groups_beside(m):
+                transpose_weights(w)
+        quantise_tokens(TOKEN_TILES - 1)
+        for w in groups_after:
+            transpose_weights(w)
+
+        for w in group_order[0 : 1 + GROUPS_PER_UNIT]:
+            quantise_weights(w)
+        for m in range(TOKEN_TILES):
+            q_and_k(m)
+        nc.sync.dma_start(out=q_view, in_=qk_sb[:, 0, :, :])
+        nc.sync.dma_start(out=k_view, in_=qk_sb[:, 1, :, :])
+        for j in range(UNITS):
+            for m in range(TOKEN_TILES):
+                geglu(j, m)
+                if j + 1 < UNITS and m < GROUPS_PER_UNIT:
+                    quantise_weights(group_order[1 + GROUPS_PER_UNIT * (j + 1) + m])

@@ -32,6 +32,7 @@ GROUPS_PER_TOKEN_TILE = (GROUPS - 1) // TOKEN_TILES
 BN_CHUNK = 512
 PSUM_BANKS = 8
 AHEAD = 2
+REORDER_ON = ("scalar", "none", "vector", "none")
 
 FLOPS = 2 * TOKENS * DIM * W_ROWS
 
@@ -50,7 +51,8 @@ def tile_latentattentionblock_pa_kernel(tc, x, norm_w, expand_w, q_out, k_out, g
         ctx.enter_context(tc.manual_schedule())
         const = ctx.enter_context(tc.tile_pool(name="const", bufs=1))
         x_pool = ctx.enter_context(tc.tile_pool(name="x_pool", bufs=TOKEN_TILES))
-        w_pool = ctx.enter_context(tc.tile_pool(name="w_pool", bufs=8))
+        w_pool = ctx.enter_context(tc.tile_pool(name="w_pool", bufs=6))
+        wo_pool = ctx.enter_context(tc.tile_pool(name="wo_pool", bufs=4))
         small = ctx.enter_context(tc.tile_pool(name="small", bufs=4))
         y_pool = ctx.enter_context(tc.tile_pool(name="y_pool", bufs=AHEAD + 1))
         h_pool = ctx.enter_context(tc.tile_pool(name="h_pool", bufs=3))
@@ -113,6 +115,18 @@ def tile_latentattentionblock_pa_kernel(tc, x, norm_w, expand_w, q_out, k_out, g
         nw_cols = const.tile([P, PASSES * PACK], F32)
         nc.vector.tensor_copy(out=nw_cols[:], in_=nw_bf[:].rearrange("p g t -> p (g t)"))
 
+        w_ordered = {}
+
+        def reorder_weights(w, engine):
+            w_ord = wo_pool.tile([P, 2, DIM], BF16)
+            src = w_raw[w][:].bitcast(F32).rearrange("p t (g j u) -> p (t g) u j", g=PASSES, u=2)
+            dst = w_ord[:].bitcast(F32).rearrange("p t (g u j) -> p (t g) u j", g=PASSES, u=2)
+            if engine == "vector":
+                nc.vector.tensor_copy(out=dst, in_=src)
+            else:
+                nc.scalar.copy(out=dst, in_=src)
+            w_ordered[w] = w_ord
+
         y_tiles = {}
         h_grouped_tiles = {}
         w_grouped_tiles = {}
@@ -165,13 +179,18 @@ def tile_latentattentionblock_pa_kernel(tc, x, norm_w, expand_w, q_out, k_out, g
             )
 
         def transpose_weights(w):
-            words = w_raw[w][:].bitcast(F32)
+            in_order = w in w_ordered
+            words = (w_ordered[w] if in_order else w_raw[w])[:].bitcast(F32)
             w_grouped = wg_pool.tile([P, PASSES, GROUP_ROWS * PACK], BF16, align_bytes=64)
             for g in range(PASSES):
                 wt = psum.tile([P, 2, 2, P], F32, tag="bank")
                 for t in range(2):
                     for u in range(2):
-                        nc.tensor.transpose(wt[:, t, u, :], words[:, t, 2 * P * g + u : 2 * P * (g + 1) : 2], ident[:])
+                        if in_order:
+                            cols = slice(2 * P * g + P * u, 2 * P * g + P * (u + 1))
+                        else:
+                            cols = slice(2 * P * g + u, 2 * P * (g + 1), 2)
+                        nc.tensor.transpose(wt[:, t, u, :], words[:, t, cols], ident[:])
                 nc.scalar.copy(
                     out=w_grouped[:, g, :].bitcast(F32).rearrange("p (r t u) -> p r t u", t=2, u=2),
                     in_=wt[:].rearrange("p t u r -> p r t u"),
@@ -216,11 +235,20 @@ def tile_latentattentionblock_pa_kernel(tc, x, norm_w, expand_w, q_out, k_out, g
             first = N_TILE * (j % 2)
             nc.sync.dma_start(out=g_views[j // 2][:, m, first : first + N_TILE], in_=prod[:])
 
+        def reorder_beside(m):
+            for w in groups_beside(m):
+                engine = REORDER_ON[group_order.index(w) % len(REORDER_ON)]
+                if engine != "none":
+                    reorder_weights(w, engine)
+
         for m in range(AHEAD):
             normalise(m)
+        reorder_beside(0)
         for m in range(TOKEN_TILES):
             if m + AHEAD < TOKEN_TILES:
                 normalise(m + AHEAD)
+            if m + 1 < TOKEN_TILES:
+                reorder_beside(m + 1)
             transpose_tokens(m)
             if m >= 1:
                 quantise_tokens(m - 1)

@@ -28,11 +28,11 @@ GROUPS = W_ROWS // GROUP_ROWS
 N_TILE = 512
 UNITS = EXP // N_TILE
 GROUPS_PER_UNIT = 2 * N_TILE // GROUP_ROWS
-GROUPS_PER_TOKEN_TILE = (GROUPS - 1) // TOKEN_TILES
+HEAD_GROUPS = 1 + GROUPS_PER_UNIT
 BN_CHUNK = 512
 PSUM_BANKS = 8
 AHEAD = 2
-REORDER_ON = ("scalar", "none", "vector", "none")
+W_BUFS = 8
 
 FLOPS = 2 * TOKENS * DIM * W_ROWS
 
@@ -51,13 +51,14 @@ def tile_latentattentionblock_pa_kernel(tc, x, norm_w, expand_w, q_out, k_out, g
         ctx.enter_context(tc.manual_schedule())
         const = ctx.enter_context(tc.tile_pool(name="const", bufs=1))
         x_pool = ctx.enter_context(tc.tile_pool(name="x_pool", bufs=TOKEN_TILES))
-        w_pool = ctx.enter_context(tc.tile_pool(name="w_pool", bufs=6))
-        wo_pool = ctx.enter_context(tc.tile_pool(name="wo_pool", bufs=4))
+        w_pool = ctx.enter_context(tc.tile_pool(name="w_pool", bufs=W_BUFS))
+        wo_pool = ctx.enter_context(tc.tile_pool(name="wo_pool", bufs=3))
         small = ctx.enter_context(tc.tile_pool(name="small", bufs=4))
         y_pool = ctx.enter_context(tc.tile_pool(name="y_pool", bufs=AHEAD + 1))
         h_pool = ctx.enter_context(tc.tile_pool(name="h_pool", bufs=3))
-        wg_pool = ctx.enter_context(tc.tile_pool(name="wg_pool", bufs=GROUPS))
-        out_pool = ctx.enter_context(tc.tile_pool(name="out_pool", bufs=4))
+        wg_pool = ctx.enter_context(tc.tile_pool(name="wg_pool", bufs=GROUPS - HEAD_GROUPS + 2))
+        gelu_pool = ctx.enter_context(tc.tile_pool(name="gelu_pool", bufs=3))
+        prod_pool = ctx.enter_context(tc.tile_pool(name="prod_pool", bufs=6))
         psum = ctx.enter_context(tc.psum_pool(name="psum", bufs=PSUM_BANKS))
 
         h_codes = const.tile([P, TOKEN_TILES, PASSES, P], U32, align_bytes=64)
@@ -68,14 +69,13 @@ def tile_latentattentionblock_pa_kernel(tc, x, norm_w, expand_w, q_out, k_out, g
 
         first_lin = 1
         first_pre = 1 + EXP // GROUP_ROWS
-        group_order = [0]
-        for j in range(UNITS):
-            group_order.extend([first_pre + 2 * j, first_pre + 2 * j + 1, first_lin + 2 * j, first_lin + 2 * j + 1])
 
-        def groups_beside(m):
-            return group_order[GROUPS_PER_TOKEN_TILE * m : GROUPS_PER_TOKEN_TILE * (m + 1)]
+        def unit_groups(j):
+            return [first_pre + 2 * j, first_pre + 2 * j + 1, first_lin + 2 * j, first_lin + 2 * j + 1]
 
-        groups_after = group_order[GROUPS_PER_TOKEN_TILE * TOKEN_TILES :]
+        group_order = unit_groups(0) + [0]
+        for j in range(1, UNITS):
+            group_order.extend(unit_groups(j))
 
         nw_bf = const.tile([P, PASSES, PACK], BF16)
         nc.scalar.dma_start(out=nw_bf[:], in_=norm_w.rearrange("(g p t) -> p g t", g=PASSES, t=PACK))
@@ -102,41 +102,33 @@ def tile_latentattentionblock_pa_kernel(tc, x, norm_w, expand_w, q_out, k_out, g
             )
             w_raw[w] = w_chunk
 
-        for m in range(AHEAD):
-            load_tokens(m)
-        for m in range(TOKEN_TILES):
-            for w in groups_beside(m):
-                load_weights(w)
-            if m + AHEAD < TOKEN_TILES:
-                load_tokens(m + AHEAD)
-        for w in groups_after:
-            load_weights(w)
+        load_tokens(0)
+        load_tokens(1)
+        for i in range(W_BUFS):
+            load_weights(group_order[i])
+            if i % 2 == 1:
+                load_tokens(2 + i // 2)
+        load_tokens(6)
+        load_tokens(7)
 
         nw_cols = const.tile([P, PASSES * PACK], F32)
         nc.vector.tensor_copy(out=nw_cols[:], in_=nw_bf[:].rearrange("p g t -> p (g t)"))
 
-        w_ordered = {}
-
-        def reorder_weights(w, engine):
-            w_ord = wo_pool.tile([P, 2, DIM], BF16)
-            src = w_raw[w][:].bitcast(F32).rearrange("p t (g j u) -> p (t g) u j", g=PASSES, u=2)
-            dst = w_ord[:].bitcast(F32).rearrange("p t (g u j) -> p (t g) u j", g=PASSES, u=2)
-            if engine == "vector":
-                nc.vector.tensor_copy(out=dst, in_=src)
-            else:
-                nc.scalar.copy(out=dst, in_=src)
-            w_ordered[w] = w_ord
-
         y_tiles = {}
         h_grouped_tiles = {}
         w_grouped_tiles = {}
+        w_ordered = {}
+        stat_tiles = {}
+
+        def stats_chunk(m, c):
+            if c == 0:
+                stats = small.tile([P, DIM // BN_CHUNK, 6], F32)
+                stat_tiles[m] = stats
+            nc.vector.bn_stats(out=stat_tiles[m][:, c, :], in_=x_raw[m][:, BN_CHUNK * c : BN_CHUNK * (c + 1)])
 
         def normalise(m):
-            stats = small.tile([P, DIM // BN_CHUNK, 6], F32)
-            for c in range(DIM // BN_CHUNK):
-                nc.vector.bn_stats(out=stats[:, c, :], in_=x_raw[m][:, BN_CHUNK * c : BN_CHUNK * (c + 1)])
             mean_var = small.tile([P, 2], F32)
-            nc.vector.bn_aggr(out=mean_var[:], in_=stats[:].rearrange("p c s -> p (c s)"))
+            nc.vector.bn_aggr(out=mean_var[:], in_=stat_tiles[m][:].rearrange("p c s -> p (c s)"))
             var_eps = small.tile([P, 1], F32)
             nc.gpsimd.tensor_scalar(out=var_eps[:], in0=mean_var[:, 1:2], scalar1=EPS, scalar2=None, op0=ALU.add)
             rstd = small.tile([P, 1], F32)
@@ -178,6 +170,14 @@ def tile_latentattentionblock_pa_kernel(tc, x, norm_w, expand_w, q_out, k_out, g
                 in_=h_grouped_tiles[m][:].rearrange("p g r t -> p (g r t)"),
             )
 
+        def reorder_weights(w):
+            w_ord = wo_pool.tile([P, 2, DIM], BF16)
+            nc.scalar.copy(
+                out=w_ord[:].bitcast(F32).rearrange("p t (g u j) -> p (t g) u j", g=PASSES, u=2),
+                in_=w_raw[w][:].bitcast(F32).rearrange("p t (g j u) -> p (t g) u j", g=PASSES, u=2),
+            )
+            w_ordered[w] = w_ord
+
         def transpose_weights(w):
             in_order = w in w_ordered
             words = (w_ordered[w] if in_order else w_raw[w])[:].bitcast(F32)
@@ -196,6 +196,9 @@ def tile_latentattentionblock_pa_kernel(tc, x, norm_w, expand_w, q_out, k_out, g
                     in_=wt[:].rearrange("p t u r -> p r t u"),
                 )
             w_grouped_tiles[w] = w_grouped
+            at = group_order.index(w)
+            if at + W_BUFS < GROUPS:
+                load_weights(group_order[at + W_BUFS])
 
         def quantise_weights(w):
             cols = slice(GROUP_ROWS * w, GROUP_ROWS * (w + 1))
@@ -223,49 +226,74 @@ def tile_latentattentionblock_pa_kernel(tc, x, norm_w, expand_w, q_out, k_out, g
             project(qk[:].rearrange("p a c -> p (a c)"), m, 0, 2 * QK)
             nc.scalar.copy(out=qk_sb[:, :, m, :], in_=qk[:])
 
-        def geglu(j, m):
+        gelu_tiles = {}
+
+        def gate(j, m):
             pre = psum.tile([P, N_TILE], F32, tag="bank")
             project(pre[:], m, 2 * QK + EXP + N_TILE * j, N_TILE)
+            gelu = gelu_pool.tile([P, N_TILE], F32)
+            nc.scalar.activation(out=gelu[:], in_=pre[:], func=ACT.Gelu)
+            gelu_tiles[(j, m)] = gelu
+
+        def product(j, m):
             lin = psum.tile([P, N_TILE], F32, tag="bank")
             project(lin[:], m, 2 * QK + N_TILE * j, N_TILE)
-            gelu = out_pool.tile([P, N_TILE], F32)
-            nc.scalar.activation(out=gelu[:], in_=pre[:], func=ACT.Gelu)
-            prod = out_pool.tile([P, N_TILE], F32)
-            nc.vector.tensor_tensor(out=prod[:], in0=lin[:], in1=gelu[:], op=ALU.mult)
+            prod = prod_pool.tile([P, N_TILE], F32)
+            nc.vector.tensor_tensor(out=prod[:], in0=lin[:], in1=gelu_tiles[(j, m)][:], op=ALU.mult)
             first = N_TILE * (j % 2)
             nc.sync.dma_start(out=g_views[j // 2][:, m, first : first + N_TILE], in_=prod[:])
 
-        def reorder_beside(m):
-            for w in groups_beside(m):
-                engine = REORDER_ON[group_order.index(w) % len(REORDER_ON)]
-                if engine != "none":
-                    reorder_weights(w, engine)
-
         for m in range(AHEAD):
+            stats_chunk(m, 0)
+            stats_chunk(m, 1)
             normalise(m)
-        reorder_beside(0)
-        for m in range(TOKEN_TILES):
-            if m + AHEAD < TOKEN_TILES:
-                normalise(m + AHEAD)
-            if m + 1 < TOKEN_TILES:
-                reorder_beside(m + 1)
-            transpose_tokens(m)
-            if m >= 1:
-                quantise_tokens(m - 1)
-            for w in groups_beside(m):
-                transpose_weights(w)
-        quantise_tokens(TOKEN_TILES - 1)
-        for w in groups_after:
-            transpose_weights(w)
+        stats_chunk(AHEAD, 0)
+        stats_chunk(AHEAD, 1)
+        transpose_weights(group_order[0])
+        transpose_weights(group_order[1])
+        transpose_tokens(0)
+        quantise_weights(group_order[0])
+        quantise_weights(group_order[1])
+        transpose_weights(group_order[2])
+        quantise_tokens(0)
+        transpose_weights(group_order[3])
+        quantise_weights(group_order[2])
+        transpose_weights(group_order[4])
+        quantise_weights(group_order[3])
+        quantise_weights(group_order[4])
+        normalise(AHEAD)
 
-        for w in group_order[0 : 1 + GROUPS_PER_UNIT]:
-            quantise_weights(w)
+        rest = group_order[HEAD_GROUPS:]
+        taken = 0
+        reorder_weights(rest[0])
         for m in range(TOKEN_TILES):
+            here = rest[taken : taken + 2 - m % 2]
+            taken += len(here)
+            if m + 1 < TOKEN_TILES:
+                transpose_tokens(m + 1)
+            gate(0, m)
             q_and_k(m)
+            if taken < len(rest):
+                reorder_weights(rest[taken])
+            if m + 1 + AHEAD < TOKEN_TILES:
+                stats_chunk(m + 1 + AHEAD, 0)
+            if m + 1 < TOKEN_TILES:
+                quantise_tokens(m + 1)
+            if 3 <= m < 3 + GROUPS_PER_UNIT:
+                quantise_weights(unit_groups(1)[m - 3])
+            if m + 1 + AHEAD < TOKEN_TILES:
+                stats_chunk(m + 1 + AHEAD, 1)
+                normalise(m + 1 + AHEAD)
+            transpose_weights(here[0])
+            product(0, m)
+            for w in here[1:]:
+                transpose_weights(w)
         nc.sync.dma_start(out=q_view, in_=qk_sb[:, 0, :, :])
         nc.sync.dma_start(out=k_view, in_=qk_sb[:, 1, :, :])
-        for j in range(UNITS):
+
+        for j in range(1, UNITS):
             for m in range(TOKEN_TILES):
-                geglu(j, m)
+                gate(j, m)
+                product(j, m)
                 if j + 1 < UNITS and m < GROUPS_PER_UNIT:
-                    quantise_weights(group_order[1 + GROUPS_PER_UNIT * (j + 1) + m])
+                    quantise_weights(unit_groups(j + 1)[m])

@@ -81,6 +81,8 @@ def tile_latentattentionblock_pa_kernel(tc, x, norm_w, expand_w, q_out, k_out, g
         nc.scalar.dma_start(out=nw_bf[:], in_=norm_w.rearrange("(g p t) -> p g t", g=PASSES, t=PACK))
         minus_half = const.tile([P, 1], F32)
         nc.vector.memset(minus_half[:], -0.5)
+        zeros = const.tile([P, N_TILE], BF16)
+        nc.vector.memset(zeros[:], 0.0)
         ident = const.tile([P, P], F32)
         make_identity(nc, ident[:])
         table_warmer = const.tile([P, 1], F32)
@@ -113,6 +115,11 @@ def tile_latentattentionblock_pa_kernel(tc, x, norm_w, expand_w, q_out, k_out, g
 
         nw_cols = const.tile([P, PASSES * PACK], F32)
         nc.vector.tensor_copy(out=nw_cols[:], in_=nw_bf[:].rearrange("p g t -> p (g t)"))
+
+        def keep_clock_up(count):
+            unread = psum.tile([P, N_TILE], F32, tag="bank")
+            for i in range(count):
+                nc.tensor.matmul(unread[:], lhsT=zeros[:, 0:P], rhs=zeros[:], start=True, stop=True)
 
         y_tiles = {}
         h_grouped_tiles = {}
@@ -249,16 +256,23 @@ def tile_latentattentionblock_pa_kernel(tc, x, norm_w, expand_w, q_out, k_out, g
             normalise(m)
         stats_chunk(AHEAD, 0)
         stats_chunk(AHEAD, 1)
+        keep_clock_up(6)
         transpose_weights(group_order[0])
+        keep_clock_up(1)
         transpose_weights(group_order[1])
+        keep_clock_up(1)
         transpose_tokens(0)
+        keep_clock_up(1)
         quantise_weights(group_order[0])
         quantise_weights(group_order[1])
         transpose_weights(group_order[2])
+        keep_clock_up(1)
         quantise_tokens(0)
         transpose_weights(group_order[3])
+        keep_clock_up(1)
         quantise_weights(group_order[2])
         transpose_weights(group_order[4])
+        keep_clock_up(1)
         quantise_weights(group_order[3])
         quantise_weights(group_order[4])
         normalise(AHEAD)
@@ -288,6 +302,7 @@ def tile_latentattentionblock_pa_kernel(tc, x, norm_w, expand_w, q_out, k_out, g
             product(0, m)
             for w in here[1:]:
                 transpose_weights(w)
+            keep_clock_up(2)
         nc.sync.dma_start(out=q_view, in_=qk_sb[:, 0, :, :])
         nc.sync.dma_start(out=k_view, in_=qk_sb[:, 1, :, :])
 

@@ -29,6 +29,7 @@ N_TILE = 512
 UNITS = EXP // N_TILE
 GROUPS_PER_UNIT = 2 * N_TILE // GROUP_ROWS
 HEAD_GROUPS = 1 + GROUPS_PER_UNIT
+BLOCKS = 2 * UNITS
 BN_CHUNK = 512
 PSUM_BANKS = 8
 AHEAD = 2
@@ -56,15 +57,17 @@ def tile_latentattentionblock_pa_kernel(tc, x, norm_w, expand_w, q_out, k_out, g
         small = ctx.enter_context(tc.tile_pool(name="small", bufs=4))
         y_pool = ctx.enter_context(tc.tile_pool(name="y_pool", bufs=AHEAD + 1))
         h_pool = ctx.enter_context(tc.tile_pool(name="h_pool", bufs=3))
-        wg_pool = ctx.enter_context(tc.tile_pool(name="wg_pool", bufs=GROUPS - HEAD_GROUPS + 2))
+        wg_pool = ctx.enter_context(tc.tile_pool(name="wg_pool", bufs=7))
         gelu_pool = ctx.enter_context(tc.tile_pool(name="gelu_pool", bufs=3))
         prod_pool = ctx.enter_context(tc.tile_pool(name="prod_pool", bufs=6))
         psum = ctx.enter_context(tc.psum_pool(name="psum", bufs=PSUM_BANKS))
 
         h_codes = const.tile([P, TOKEN_TILES, PASSES, P], U32, align_bytes=64)
         h_scales = const.tile([P, TOKEN_TILES, PASSES, P], U8, align_bytes=64)
-        w_codes = const.tile([P, PASSES, W_ROWS], U32, align_bytes=64)
-        w_scales = const.tile([P, PASSES, W_ROWS], U8, align_bytes=64)
+        w_codes = const.tile([P, BLOCKS, PASSES, N_TILE], U32, align_bytes=64)
+        w_scales = const.tile([P, BLOCKS, PASSES, N_TILE], U8, align_bytes=64)
+        qk_codes = const.tile([P, PASSES, GROUP_ROWS], U32, align_bytes=64)
+        qk_scales = const.tile([P, PASSES, GROUP_ROWS], U8, align_bytes=64)
         qk_sb = const.tile([P, 2, TOKEN_TILES, QK], F32)
 
         first_lin = 1
@@ -188,7 +191,13 @@ def tile_latentattentionblock_pa_kernel(tc, x, norm_w, expand_w, q_out, k_out, g
         def transpose_weights(w):
             in_order = w in w_ordered
             words = (w_ordered[w] if in_order else w_raw[w])[:].bitcast(F32)
-            w_grouped = wg_pool.tile([P, PASSES, GROUP_ROWS * PACK], BF16, align_bytes=64)
+            half = (w - 1) % 2 if w > 0 else 0
+            if half == 0:
+                w_grouped = wg_pool.tile([P, PASSES, (2 if w > 0 else 1) * GROUP_ROWS * PACK], BF16, align_bytes=64)
+                w_grouped_tiles[w] = w_grouped
+            else:
+                w_grouped = w_grouped_tiles[w - 1]
+            cols_out = slice(half * GROUP_ROWS * PACK, (half + 1) * GROUP_ROWS * PACK)
             for g in range(PASSES):
                 wt = psum.tile([P, 2, 2, P], F32, tag="bank")
                 for t in range(2):
@@ -199,56 +208,75 @@ def tile_latentattentionblock_pa_kernel(tc, x, norm_w, expand_w, q_out, k_out, g
                             cols = slice(2 * P * g + u, 2 * P * (g + 1), 2)
                         nc.tensor.transpose(wt[:, t, u, :], words[:, t, cols], ident[:])
                 nc.scalar.copy(
-                    out=w_grouped[:, g, :].bitcast(F32).rearrange("p (r t u) -> p r t u", t=2, u=2),
+                    out=w_grouped[:, g, cols_out].bitcast(F32).rearrange("p (r t u) -> p r t u", t=2, u=2),
                     in_=wt[:].rearrange("p t u r -> p r t u"),
                 )
-            w_grouped_tiles[w] = w_grouped
             at = group_order.index(w)
             if at + W_BUFS < GROUPS:
                 load_weights(group_order[at + W_BUFS])
 
-        def quantise_weights(w):
-            cols = slice(GROUP_ROWS * w, GROUP_ROWS * (w + 1))
-            for g in range(PASSES):
-                nc.vector.quantize_mx(
-                    out=w_codes[:, g, cols].bitcast(FP8X4),
-                    scales=w_scales[:, g, cols],
-                    in_=w_grouped_tiles[w][:, g, :],
-                )
+        def quantise_head_columns():
+            nc.vector.quantize_mx(
+                out=qk_codes[:].rearrange("p g r -> p (g r)").bitcast(FP8X4),
+                scales=qk_scales[:].rearrange("p g r -> p (g r)"),
+                in_=w_grouped_tiles[0][:].rearrange("p g r -> p (g r)"),
+            )
 
-        def project(acc, m, first, width):
+        def quantise_block(b):
+            nc.vector.quantize_mx(
+                out=w_codes[:, b, :, :].rearrange("p g r -> p (g r)").bitcast(FP8X4),
+                scales=w_scales[:, b, :, :].rearrange("p g r -> p (g r)"),
+                in_=w_grouped_tiles[1 + 2 * b][:].rearrange("p g r -> p (g r)"),
+            )
+
+        def project(acc, m, codes, scales):
             for g in range(PASSES):
                 nc.tensor.matmul_mx(
                     out=acc,
                     lhsT=h_codes[:, m, g, :].bitcast(FP8X4),
                     lhsT_scale=h_scales[:, m, g, :],
-                    rhs=w_codes[:, g, first : first + width].bitcast(FP8X4),
-                    rhs_scale=w_scales[:, g, first : first + width],
+                    rhs=codes[:, g, :].bitcast(FP8X4),
+                    rhs_scale=scales[:, g, :],
                     start=(g == 0),
                     stop=(g == PASSES - 1),
                 )
 
         def q_and_k(m):
             qk = psum.tile([P, 2, QK], F32, tag="bank")
-            project(qk[:].rearrange("p a c -> p (a c)"), m, 0, 2 * QK)
+            project(qk[:].rearrange("p a c -> p (a c)"), m, qk_codes, qk_scales)
             nc.scalar.copy(out=qk_sb[:, :, m, :], in_=qk[:])
 
         gelu_tiles = {}
 
         def gate(j, m):
             pre = psum.tile([P, N_TILE], F32, tag="bank")
-            project(pre[:], m, 2 * QK + EXP + N_TILE * j, N_TILE)
+            project(pre[:], m, w_codes[:, UNITS + j, :, :], w_scales[:, UNITS + j, :, :])
             gelu = gelu_pool.tile([P, N_TILE], F32)
             nc.scalar.activation(out=gelu[:], in_=pre[:], func=ACT.Gelu)
             gelu_tiles[(j, m)] = gelu
 
         def product(j, m):
             lin = psum.tile([P, N_TILE], F32, tag="bank")
-            project(lin[:], m, 2 * QK + N_TILE * j, N_TILE)
+            project(lin[:], m, w_codes[:, j, :, :], w_scales[:, j, :, :])
             prod = prod_pool.tile([P, N_TILE], F32)
             nc.vector.tensor_tensor(out=prod[:], in0=lin[:], in1=gelu_tiles[(j, m)][:], op=ALU.mult)
             first = N_TILE * (j % 2)
             nc.sync.dma_start(out=g_views[j // 2][:, m, first : first + N_TILE], in_=prod[:])
+
+        def last_cell(j, m):
+            width = N_TILE // 2
+            for half in range(2):
+                cols = slice(width * half, width * (half + 1))
+                pre = psum.tile([P, N_TILE], F32, tag="bank")
+                project(pre[:, 0:width], m, w_codes[:, UNITS + j, :, cols], w_scales[:, UNITS + j, :, cols])
+                gelu = gelu_pool.tile([P, N_TILE], F32)
+                nc.scalar.activation(out=gelu[:, 0:width], in_=pre[:, 0:width], func=ACT.Gelu)
+                lin = psum.tile([P, N_TILE], F32, tag="bank")
+                project(lin[:, 0:width], m, w_codes[:, j, :, cols], w_scales[:, j, :, cols])
+                prod = prod_pool.tile([P, N_TILE], F32)
+                nc.vector.tensor_tensor(out=prod[:, 0:width], in0=lin[:, 0:width], in1=gelu[:, 0:width], op=ALU.mult)
+                first = N_TILE * (j % 2) + width * half
+                nc.sync.dma_start(out=g_views[j // 2][:, m, first : first + width], in_=prod[:, 0:width])
 
         for m in range(AHEAD):
             stats_chunk(m, 0)
@@ -256,25 +284,23 @@ def tile_latentattentionblock_pa_kernel(tc, x, norm_w, expand_w, q_out, k_out, g
             normalise(m)
         stats_chunk(AHEAD, 0)
         stats_chunk(AHEAD, 1)
-        keep_clock_up(6)
+        keep_clock_up(5)
         transpose_weights(group_order[0])
         keep_clock_up(1)
         transpose_weights(group_order[1])
         keep_clock_up(1)
         transpose_tokens(0)
         keep_clock_up(1)
-        quantise_weights(group_order[0])
-        quantise_weights(group_order[1])
+        quantise_block(UNITS)
         transpose_weights(group_order[2])
         keep_clock_up(1)
         quantise_tokens(0)
         transpose_weights(group_order[3])
         keep_clock_up(1)
-        quantise_weights(group_order[2])
         transpose_weights(group_order[4])
         keep_clock_up(1)
-        quantise_weights(group_order[3])
-        quantise_weights(group_order[4])
+        quantise_block(0)
+        quantise_head_columns()
         normalise(AHEAD)
 
         rest = group_order[HEAD_GROUPS:]
@@ -293,8 +319,10 @@ def tile_latentattentionblock_pa_kernel(tc, x, norm_w, expand_w, q_out, k_out, g
                 stats_chunk(m + 1 + AHEAD, 0)
             if m + 1 < TOKEN_TILES:
                 quantise_tokens(m + 1)
-            if 3 <= m < 3 + GROUPS_PER_UNIT:
-                quantise_weights(unit_groups(1)[m - 3])
+            if m == 4:
+                quantise_block(UNITS + 1)
+            if m == 6:
+                quantise_block(1)
             if m + 1 + AHEAD < TOKEN_TILES:
                 stats_chunk(m + 1 + AHEAD, 1)
                 normalise(m + 1 + AHEAD)
@@ -302,13 +330,17 @@ def tile_latentattentionblock_pa_kernel(tc, x, norm_w, expand_w, q_out, k_out, g
             product(0, m)
             for w in here[1:]:
                 transpose_weights(w)
-            keep_clock_up(2)
         nc.sync.dma_start(out=q_view, in_=qk_sb[:, 0, :, :])
         nc.sync.dma_start(out=k_view, in_=qk_sb[:, 1, :, :])
 
         for j in range(1, UNITS):
             for m in range(TOKEN_TILES):
-                gate(j, m)
-                product(j, m)
-                if j + 1 < UNITS and m < GROUPS_PER_UNIT:
-                    quantise_weights(unit_groups(j + 1)[m])
+                if j == UNITS - 1 and m == TOKEN_TILES - 1:
+                    last_cell(j, m)
+                else:
+                    gate(j, m)
+                    product(j, m)
+                if j + 1 < UNITS and m == 0:
+                    quantise_block(UNITS + j + 1)
+                if j + 1 < UNITS and m == 3:
+                    quantise_block(j + 1)

@@ -32,6 +32,7 @@ HEAD_GROUPS = 1 + GROUPS_PER_UNIT
 BLOCKS = 2 * UNITS
 BN_CHUNK = 512
 PSUM_BANKS = 8
+STEP_GROUPS = (2, 1, 2, 1, 2, 2, 1, 1)
 AHEAD = 2
 W_BUFS = 8
 
@@ -58,7 +59,7 @@ def tile_latentattentionblock_pa_kernel(tc, x, norm_w, expand_w, q_out, k_out, g
         y_pool = ctx.enter_context(tc.tile_pool(name="y_pool", bufs=AHEAD + 1))
         h_pool = ctx.enter_context(tc.tile_pool(name="h_pool", bufs=3))
         wg_pool = ctx.enter_context(tc.tile_pool(name="wg_pool", bufs=7))
-        gelu_pool = ctx.enter_context(tc.tile_pool(name="gelu_pool", bufs=3))
+        gelu_pool = ctx.enter_context(tc.tile_pool(name="gelu_pool", bufs=5))
         prod_pool = ctx.enter_context(tc.tile_pool(name="prod_pool", bufs=6))
         psum = ctx.enter_context(tc.psum_pool(name="psum", bufs=PSUM_BANKS))
 
@@ -108,13 +109,20 @@ def tile_latentattentionblock_pa_kernel(tc, x, norm_w, expand_w, q_out, k_out, g
             w_raw[w] = w_chunk
 
         load_tokens(0)
+        load_weights(group_order[0])
+        load_weights(group_order[1])
         load_tokens(1)
-        for i in range(W_BUFS):
-            load_weights(group_order[i])
-            if i % 2 == 1:
-                load_tokens(2 + i // 2)
-        load_tokens(6)
-        load_tokens(7)
+        load_weights(group_order[2])
+        load_tokens(2)
+        load_weights(group_order[3])
+        load_tokens(3)
+        load_weights(group_order[4])
+        load_weights(group_order[5])
+        load_tokens(4)
+        load_weights(group_order[6])
+        load_weights(group_order[7])
+        for m in range(5, TOKEN_TILES):
+            load_tokens(m)
 
         nw_cols = const.tile([P, PASSES * PACK], F32)
         nc.vector.tensor_copy(out=nw_cols[:], in_=nw_bf[:].rearrange("p g t -> p (g t)"))
@@ -307,21 +315,21 @@ def tile_latentattentionblock_pa_kernel(tc, x, norm_w, expand_w, q_out, k_out, g
         taken = 0
         reorder_weights(rest[0])
         for m in range(TOKEN_TILES):
-            here = rest[taken : taken + 2 - m % 2]
+            here = rest[taken : taken + STEP_GROUPS[m]]
             taken += len(here)
             if m + 1 < TOKEN_TILES:
                 transpose_tokens(m + 1)
             gate(0, m)
             q_and_k(m)
-            if taken < len(rest):
+            if taken < len(rest) and m != 5:
                 reorder_weights(rest[taken])
             if m + 1 + AHEAD < TOKEN_TILES:
                 stats_chunk(m + 1 + AHEAD, 0)
             if m + 1 < TOKEN_TILES:
                 quantise_tokens(m + 1)
-            if m == 4:
-                quantise_block(UNITS + 1)
             if m == 6:
+                quantise_block(UNITS + 1)
+            if m == 7:
                 quantise_block(1)
             if m + 1 + AHEAD < TOKEN_TILES:
                 stats_chunk(m + 1 + AHEAD, 1)

@@ -32,7 +32,9 @@ HEAD_GROUPS = 1 + GROUPS_PER_UNIT
 BLOCKS = 2 * UNITS
 BN_CHUNK = 512
 PSUM_BANKS = 8
-STEP_GROUPS = (2, 1, 2, 1, 2, 2, 1, 1)
+QK_TILES = ((), (), (0, 1), (2, 3), (4,), (5,), (6,), (7,))
+STEP_GROUPS = (2, 2, 1, 1, 2, 2, 1, 1)
+SCALAR_STATS = (4,)
 AHEAD = 2
 W_BUFS = 8
 
@@ -55,7 +57,8 @@ def tile_latentattentionblock_pa_kernel(tc, x, norm_w, expand_w, q_out, k_out, g
         x_pool = ctx.enter_context(tc.tile_pool(name="x_pool", bufs=TOKEN_TILES))
         w_pool = ctx.enter_context(tc.tile_pool(name="w_pool", bufs=W_BUFS))
         wo_pool = ctx.enter_context(tc.tile_pool(name="wo_pool", bufs=3))
-        small = ctx.enter_context(tc.tile_pool(name="small", bufs=4))
+        small = ctx.enter_context(tc.tile_pool(name="small", bufs=8))
+        unread_pool = ctx.enter_context(tc.tile_pool(name="unread_pool", bufs=1))
         y_pool = ctx.enter_context(tc.tile_pool(name="y_pool", bufs=AHEAD + 1))
         h_pool = ctx.enter_context(tc.tile_pool(name="h_pool", bufs=3))
         wg_pool = ctx.enter_context(tc.tile_pool(name="wg_pool", bufs=7))
@@ -108,21 +111,11 @@ def tile_latentattentionblock_pa_kernel(tc, x, norm_w, expand_w, q_out, k_out, g
             )
             w_raw[w] = w_chunk
 
-        load_tokens(0)
-        load_weights(group_order[0])
-        load_weights(group_order[1])
-        load_tokens(1)
-        load_weights(group_order[2])
-        load_tokens(2)
-        load_weights(group_order[3])
-        load_tokens(3)
-        load_weights(group_order[4])
-        load_weights(group_order[5])
-        load_tokens(4)
-        load_weights(group_order[6])
-        load_weights(group_order[7])
-        for m in range(5, TOKEN_TILES):
-            load_tokens(m)
+        for kind, i in [["x",0],["w",0],["w",1],["x",1],["w",2],["x",2],["w",3],["w",4],["x",3],["w",5],["x",4],["w",6],["w",7],["x",5],["x",6],["x",7]]:
+            if kind == "x":
+                load_tokens(i)
+            else:
+                load_weights(group_order[i])
 
         nw_cols = const.tile([P, PASSES * PACK], F32)
         nc.vector.tensor_copy(out=nw_cols[:], in_=nw_bf[:].rearrange("p g t -> p (g t)"))
@@ -139,22 +132,46 @@ def tile_latentattentionblock_pa_kernel(tc, x, norm_w, expand_w, q_out, k_out, g
         stat_tiles = {}
 
         def stats_chunk(m, c):
+            if m in SCALAR_STATS:
+                return
             if c == 0:
                 stats = small.tile([P, DIM // BN_CHUNK, 6], F32)
                 stat_tiles[m] = stats
             nc.vector.bn_stats(out=stat_tiles[m][:, c, :], in_=x_raw[m][:, BN_CHUNK * c : BN_CHUNK * (c + 1)])
 
+        sums = {}
+
+        def scalar_stats(m, which):
+            total = small.tile([P, 1], F32, tag="total")
+            unread = unread_pool.tile([P, DIM], BF16)
+            nc.scalar.activation(
+                out=unread[:], in_=x_raw[m][:], func=ACT.Square if which else ACT.Identity, accum_out=total[:]
+            )
+            sums[(m, which)] = total
+
         def normalise(m):
-            mean_var = small.tile([P, 2], F32)
-            nc.vector.bn_aggr(out=mean_var[:], in_=stat_tiles[m][:].rearrange("p c s -> p (c s)"))
+            minus_mean = small.tile([P, 1], F32)
             var_eps = small.tile([P, 1], F32)
-            nc.gpsimd.tensor_scalar(out=var_eps[:], in0=mean_var[:, 1:2], scalar1=EPS, scalar2=None, op0=ALU.add)
+            if m in SCALAR_STATS:
+                square_eps = small.tile([P, 1], F32)
+                nc.gpsimd.tensor_scalar(
+                    out=minus_mean[:], in0=sums[(m, 0)][:], scalar1=-1.0 / DIM, scalar2=0.0, op0=ALU.mult, op1=ALU.add
+                )
+                nc.gpsimd.tensor_scalar(
+                    out=square_eps[:], in0=sums[(m, 1)][:], scalar1=1.0 / DIM, scalar2=EPS, op0=ALU.mult, op1=ALU.add
+                )
+                mean_square = small.tile([P, 1], F32)
+                nc.gpsimd.tensor_tensor(out=mean_square[:], in0=minus_mean[:], in1=minus_mean[:], op=ALU.mult)
+                nc.gpsimd.tensor_tensor(out=var_eps[:], in0=square_eps[:], in1=mean_square[:], op=ALU.subtract)
+            else:
+                mean_var = small.tile([P, 2], F32)
+                nc.vector.bn_aggr(out=mean_var[:], in_=stat_tiles[m][:].rearrange("p c s -> p (c s)"))
+                nc.gpsimd.tensor_scalar(out=var_eps[:], in0=mean_var[:, 1:2], scalar1=EPS, scalar2=None, op0=ALU.add)
+                nc.gpsimd.tensor_scalar(
+                    out=minus_mean[:], in0=mean_var[:, 0:1], scalar1=-1.0, scalar2=0.0, op0=ALU.mult, op1=ALU.add
+                )
             rstd = small.tile([P, 1], F32)
             nc.gpsimd.tensor_tensor(out=rstd[:], in0=var_eps[:], in1=minus_half[:], op=ALU.pow)
-            minus_mean = small.tile([P, 1], F32)
-            nc.gpsimd.tensor_scalar(
-                out=minus_mean[:], in0=mean_var[:, 0:1], scalar1=-1.0, scalar2=0.0, op0=ALU.mult, op1=ALU.add
-            )
             y = y_pool.tile([P, PACK, DIM // PACK], F32)
             nc.gpsimd.tensor_scalar(
                 out=y[:],
@@ -290,43 +307,42 @@ def tile_latentattentionblock_pa_kernel(tc, x, norm_w, expand_w, q_out, k_out, g
             stats_chunk(m, 0)
             stats_chunk(m, 1)
             normalise(m)
-        stats_chunk(AHEAD, 0)
-        stats_chunk(AHEAD, 1)
         keep_clock_up(5)
         transpose_weights(group_order[0])
-        keep_clock_up(1)
         transpose_weights(group_order[1])
         keep_clock_up(1)
         transpose_tokens(0)
-        keep_clock_up(1)
+        stats_chunk(AHEAD, 0)
+        stats_chunk(AHEAD, 1)
         quantise_block(UNITS)
         transpose_weights(group_order[2])
         keep_clock_up(1)
         quantise_tokens(0)
         transpose_weights(group_order[3])
-        keep_clock_up(1)
         transpose_weights(group_order[4])
-        keep_clock_up(1)
         quantise_block(0)
-        quantise_head_columns()
         normalise(AHEAD)
 
         rest = group_order[HEAD_GROUPS:]
         taken = 0
-        reorder_weights(rest[0])
         for m in range(TOKEN_TILES):
             here = rest[taken : taken + STEP_GROUPS[m]]
             taken += len(here)
             if m + 1 < TOKEN_TILES:
                 transpose_tokens(m + 1)
             gate(0, m)
-            q_and_k(m)
-            if taken < len(rest) and m != 5:
+            for i in QK_TILES[m]:
+                q_and_k(i)
+            if m < 2:
+                scalar_stats(4, m)
+            elif m in (2, 3, 4, 6):
                 reorder_weights(rest[taken])
             if m + 1 + AHEAD < TOKEN_TILES:
                 stats_chunk(m + 1 + AHEAD, 0)
             if m + 1 < TOKEN_TILES:
                 quantise_tokens(m + 1)
+            if m == 1:
+                quantise_head_columns()
             if m == 6:
                 quantise_block(UNITS + 1)
             if m == 7:

@@ -32,6 +32,7 @@ HEAD_GROUPS = 1 + GROUPS_PER_UNIT
 BLOCKS = 2 * UNITS
 BN_CHUNK = 512
 PSUM_BANKS = 8
+LAST_WIDTHS = (N_TILE // 2, N_TILE // 2)
 QK_TILES = ((), (), (0, 1), (2, 3), (4,), (5,), (6,), (7,))
 STEP_GROUPS = (2, 2, 1, 1, 2, 2, 1, 1)
 SCALAR_STATS = (4,)
@@ -66,12 +67,12 @@ def tile_latentattentionblock_pa_kernel(tc, x, norm_w, expand_w, q_out, k_out, g
         prod_pool = ctx.enter_context(tc.tile_pool(name="prod_pool", bufs=6))
         psum = ctx.enter_context(tc.psum_pool(name="psum", bufs=PSUM_BANKS))
 
-        h_codes = const.tile([P, TOKEN_TILES, PASSES, P], U32, align_bytes=64)
-        h_scales = const.tile([P, TOKEN_TILES, PASSES, P], U8, align_bytes=64)
-        w_codes = const.tile([P, BLOCKS, PASSES, N_TILE], U32, align_bytes=64)
-        w_scales = const.tile([P, BLOCKS, PASSES, N_TILE], U8, align_bytes=64)
-        qk_codes = const.tile([P, PASSES, GROUP_ROWS], U32, align_bytes=64)
-        qk_scales = const.tile([P, PASSES, GROUP_ROWS], U8, align_bytes=64)
+        h_codes = const.tile([P, TOKEN_TILES, PASSES, P], U32, align_bytes=256)
+        h_scales = const.tile([P, TOKEN_TILES, PASSES, P], U8, align_bytes=256)
+        w_codes = const.tile([P, BLOCKS, PASSES, N_TILE], U32, align_bytes=256)
+        w_scales = const.tile([P, BLOCKS, PASSES, N_TILE], U8, align_bytes=256)
+        qk_codes = const.tile([P, PASSES, GROUP_ROWS], U32, align_bytes=256)
+        qk_scales = const.tile([P, PASSES, GROUP_ROWS], U8, align_bytes=256)
         qk_sb = const.tile([P, 2, TOKEN_TILES, QK], F32)
 
         first_lin = 1
@@ -289,19 +290,23 @@ def tile_latentattentionblock_pa_kernel(tc, x, norm_w, expand_w, q_out, k_out, g
             nc.sync.dma_start(out=g_views[j // 2][:, m, first : first + N_TILE], in_=prod[:])
 
         def last_cell(j, m):
-            width = N_TILE // 2
-            for half in range(2):
-                cols = slice(width * half, width * (half + 1))
+            firsts = [sum(LAST_WIDTHS[:i]) for i in range(len(LAST_WIDTHS))]
+            parts = []
+            for first, width in zip(firsts, LAST_WIDTHS):
+                cols = slice(first, first + width)
                 pre = psum.tile([P, N_TILE], F32, tag="bank")
                 project(pre[:, 0:width], m, w_codes[:, UNITS + j, :, cols], w_scales[:, UNITS + j, :, cols])
                 gelu = gelu_pool.tile([P, N_TILE], F32)
                 nc.scalar.activation(out=gelu[:, 0:width], in_=pre[:, 0:width], func=ACT.Gelu)
+                parts.append(gelu)
+            for first, width, gelu in zip(firsts, LAST_WIDTHS, parts):
+                cols = slice(first, first + width)
                 lin = psum.tile([P, N_TILE], F32, tag="bank")
                 project(lin[:, 0:width], m, w_codes[:, j, :, cols], w_scales[:, j, :, cols])
                 prod = prod_pool.tile([P, N_TILE], F32)
                 nc.vector.tensor_tensor(out=prod[:, 0:width], in0=lin[:, 0:width], in1=gelu[:, 0:width], op=ALU.mult)
-                first = N_TILE * (j % 2) + width * half
-                nc.sync.dma_start(out=g_views[j // 2][:, m, first : first + width], in_=prod[:, 0:width])
+                first_out = N_TILE * (j % 2) + first
+                nc.sync.dma_start(out=g_views[j // 2][:, m, first_out : first_out + width], in_=prod[:, 0:width])
 
         for m in range(AHEAD):
             stats_chunk(m, 0)

from contextlib import ExitStack

import concourse.mybir as mybir
from concourse.masks import make_identity

F32 = mybir.dt.float32
BF16 = mybir.dt.bfloat16
U32 = mybir.dt.uint32
U8 = mybir.dt.uint8
FP8X4 = mybir.dt.float8_e4m3fn_x4
ACT = mybir.ActivationFunctionType
ALU = mybir.AluOpType

P = 128
TOKENS = 1024
DIM = 1024
QK = 128
EXP = 2048
W_ROWS = 2 * QK + 2 * EXP
EPS = 1e-5

PACK = 4
K_PASS = P * PACK
PASSES = DIM // K_PASS
TOKEN_TILES = TOKENS // P
GROUP_ROWS = 2 * P
GROUPS = W_ROWS // GROUP_ROWS
N_TILE = 512
UNITS = EXP // N_TILE
GROUPS_PER_UNIT = 2 * N_TILE // GROUP_ROWS
HEAD_GROUPS = 1 + GROUPS_PER_UNIT
BLOCKS = 2 * UNITS
BN_CHUNK = 512
PSUM_BANKS = 8
LAST_WIDTHS = (N_TILE // 2, N_TILE // 2)
QK_TILES = ((), (), (0, 1), (2, 3), (4,), (5,), (6,), (7,))
STEP_GROUPS = (2, 2, 1, 1, 2, 2, 1, 1)
SCALAR_STATS = (4,)
AHEAD = 2
W_BUFS = 8

FLOPS = 2 * TOKENS * DIM * W_ROWS


def tile_latentattentionblock_pa_kernel(tc, x, norm_w, expand_w, q_out, k_out, gl_out, gv_out):
    nc = tc.nc
    x_view = x.rearrange("b (p m) k -> p (b m) k", m=TOKEN_TILES)
    q_view = q_out.rearrange("b (p m) c -> p (b m) c", m=TOKEN_TILES)
    k_view = k_out.rearrange("b (p m) c -> p (b m) c", m=TOKEN_TILES)
    g_views = [
        gl_out.rearrange("b (p m) c -> p (b m) c", m=TOKEN_TILES),
        gv_out.rearrange("b (p m) c -> p (b m) c", m=TOKEN_TILES),
    ]

    with ExitStack() as ctx:
        ctx.enter_context(tc.manual_schedule())
        const = ctx.enter_context(tc.tile_pool(name="const", bufs=1))
        x_pool = ctx.enter_context(tc.tile_pool(name="x_pool", bufs=TOKEN_TILES))
        w_pool = ctx.enter_context(tc.tile_pool(name="w_pool", bufs=W_BUFS))
        wo_pool = ctx.enter_context(tc.tile_pool(name="wo_pool", bufs=3))
        small = ctx.enter_context(tc.tile_pool(name="small", bufs=8))
        unread_pool = ctx.enter_context(tc.tile_pool(name="unread_pool", bufs=1))
        y_pool = ctx.enter_context(tc.tile_pool(name="y_pool", bufs=AHEAD + 1))
        h_pool = ctx.enter_context(tc.tile_pool(name="h_pool", bufs=3))
        wg_pool = ctx.enter_context(tc.tile_pool(name="wg_pool", bufs=7))
        gelu_pool = ctx.enter_context(tc.tile_pool(name="gelu_pool", bufs=5))
        prod_pool = ctx.enter_context(tc.tile_pool(name="prod_pool", bufs=6))
        psum = ctx.enter_context(tc.psum_pool(name="psum", bufs=PSUM_BANKS))

        h_codes = const.tile([P, TOKEN_TILES, PASSES, P], U32, align_bytes=256)
        h_scales = const.tile([P, TOKEN_TILES, PASSES, P], U8, align_bytes=256)
        w_codes = const.tile([P, BLOCKS, PASSES, N_TILE], U32, align_bytes=256)
        w_scales = const.tile([P, BLOCKS, PASSES, N_TILE], U8, align_bytes=256)
        qk_codes = const.tile([P, PASSES, GROUP_ROWS], U32, align_bytes=256)
        qk_scales = const.tile([P, PASSES, GROUP_ROWS], U8, align_bytes=256)
        qk_sb = const.tile([P, 2, TOKEN_TILES, QK], F32)

        first_lin = 1
        first_pre = 1 + EXP // GROUP_ROWS

        def unit_groups(j):
            return [first_pre + 2 * j, first_pre + 2 * j + 1, first_lin + 2 * j, first_lin + 2 * j + 1]

        group_order = unit_groups(0) + [0]
        for j in range(1, UNITS):
            group_order.extend(unit_groups(j))

        nw_bf = const.tile([P, PASSES, PACK], BF16)
        nc.scalar.dma_start(out=nw_bf[:], in_=norm_w.rearrange("(g p t) -> p g t", g=PASSES, t=PACK))
        minus_half = const.tile([P, 1], F32)
        nc.vector.memset(minus_half[:], -0.5)
        zeros = const.tile([P, N_TILE], BF16)
        nc.vector.memset(zeros[:], 0.0)
        ident = const.tile([P, P], F32)
        make_identity(nc, ident[:])
        table_warmer = const.tile([P, 1], F32)
        nc.scalar.activation(out=table_warmer[:], in_=minus_half[:], func=ACT.Gelu)

        x_raw = {}
        w_raw = {}

        def load_tokens(m):
            x_tile = x_pool.tile([P, DIM], BF16)
            nc.sync.dma_start(out=x_tile[:], in_=x_view[:, m, :])
            x_raw[m] = x_tile

        def load_weights(w):
            w_chunk = w_pool.tile([P, 2, DIM], BF16)
            nc.sync.dma_start(
                out=w_chunk[:],
                in_=expand_w[GROUP_ROWS * w : GROUP_ROWS * (w + 1), :].rearrange("(p t) k -> p t k", t=2),
            )
            w_raw[w] = w_chunk

        for kind, i in [["x",0],["w",0],["w",1],["x",1],["w",2],["x",2],["w",3],["w",4],["x",3],["w",5],["x",4],["w",6],["w",7],["x",5],["x",6],["x",7]]:
            if kind == "x":
                load_tokens(i)
            else:
                load_weights(group_order[i])

        nw_cols = const.tile([P, PASSES * PACK], F32)
        nc.vector.tensor_copy(out=nw_cols[:], in_=nw_bf[:].rearrange("p g t -> p (g t)"))

        def keep_clock_up(count):
            unread = psum.tile([P, N_TILE], F32, tag="bank")
            for i in range(count):
                nc.tensor.matmul(unread[:], lhsT=zeros[:, 0:P], rhs=zeros[:], start=True, stop=True)

        y_tiles = {}
        h_grouped_tiles = {}
        w_grouped_tiles = {}
        w_ordered = {}
        stat_tiles = {}

        def stats_chunk(m, c):
            if m in SCALAR_STATS:
                return
            if c == 0:
                stats = small.tile([P, DIM // BN_CHUNK, 6], F32)
                stat_tiles[m] = stats
            nc.vector.bn_stats(out=stat_tiles[m][:, c, :], in_=x_raw[m][:, BN_CHUNK * c : BN_CHUNK * (c + 1)])

        sums = {}

        def scalar_stats(m, which):
            total = small.tile([P, 1], F32, tag="total")
            unread = unread_pool.tile([P, DIM], BF16)
            nc.scalar.activation(
                out=unread[:], in_=x_raw[m][:], func=ACT.Square if which else ACT.Identity, accum_out=total[:]
            )
            sums[(m, which)] = total

        def normalise(m):
            minus_mean = small.tile([P, 1], F32)
            var_eps = small.tile([P, 1], F32)
            if m in SCALAR_STATS:
                square_eps = small.tile([P, 1], F32)
                nc.gpsimd.tensor_scalar(
                    out=minus_mean[:], in0=sums[(m, 0)][:], scalar1=-1.0 / DIM, scalar2=0.0, op0=ALU.mult, op1=ALU.add
                )
                nc.gpsimd.tensor_scalar(
                    out=square_eps[:], in0=sums[(m, 1)][:], scalar1=1.0 / DIM, scalar2=EPS, op0=ALU.mult, op1=ALU.add
                )
                mean_square = small.tile([P, 1], F32)
                nc.gpsimd.tensor_tensor(out=mean_square[:], in0=minus_mean[:], in1=minus_mean[:], op=ALU.mult)
                nc.gpsimd.tensor_tensor(out=var_eps[:], in0=square_eps[:], in1=mean_square[:], op=ALU.subtract)
            else:
                mean_var = small.tile([P, 2], F32)
                nc.vector.bn_aggr(out=mean_var[:], in_=stat_tiles[m][:].rearrange("p c s -> p (c s)"))
                nc.gpsimd.tensor_scalar(out=var_eps[:], in0=mean_var[:, 1:2], scalar1=EPS, scalar2=None, op0=ALU.add)
                nc.gpsimd.tensor_scalar(
                    out=minus_mean[:], in0=mean_var[:, 0:1], scalar1=-1.0, scalar2=0.0, op0=ALU.mult, op1=ALU.add
                )
            rstd = small.tile([P, 1], F32)
            nc.gpsimd.tensor_tensor(out=rstd[:], in0=var_eps[:], in1=minus_half[:], op=ALU.pow)
            y = y_pool.tile([P, PACK, DIM // PACK], F32)
            nc.gpsimd.tensor_scalar(
                out=y[:],
                in0=x_raw[m][:].rearrange("p (j t) -> p t j", t=PACK),
                scalar1=minus_mean[:, 0:1],
                scalar2=rstd[:, 0:1],
                op0=ALU.add,
                op1=ALU.mult,
            )
            y_tiles[m] = y

        def transpose_tokens(m):
            y = y_tiles[m]
            h_grouped = h_pool.tile([P, PASSES, P, PACK], BF16, align_bytes=64)
            for g in range(PASSES):
                yt = psum.tile([P, PACK, P], F32, tag="bank")
                for t in range(PACK):
                    nc.tensor.transpose(yt[:, t, :], y[:, t, P * g : P * (g + 1)], ident[:])
                nc.vector.tensor_tensor(
                    out=h_grouped[:, g, :, :],
                    in0=yt[:].rearrange("p t r -> p r t"),
                    in1=nw_cols[:, PACK * g : PACK * (g + 1)].unsqueeze(1).to_broadcast([P, P, PACK]),
                    op=ALU.mult,
                )
            h_grouped_tiles[m] = h_grouped

        def quantise_tokens(m):
            nc.vector.quantize_mx(
                out=h_codes[:, m, :, :].rearrange("p g r -> p (g r)").bitcast(FP8X4),
                scales=h_scales[:, m, :, :].rearrange("p g r -> p (g r)"),
                in_=h_grouped_tiles[m][:].rearrange("p g r t -> p (g r t)"),
            )

        def reorder_weights(w):
            w_ord = wo_pool.tile([P, 2, DIM], BF16)
            nc.scalar.copy(
                out=w_ord[:].bitcast(F32).rearrange("p t (g u j) -> p (t g) u j", g=PASSES, u=2),
                in_=w_raw[w][:].bitcast(F32).rearrange("p t (g j u) -> p (t g) u j", g=PASSES, u=2),
            )
            w_ordered[w] = w_ord

        def transpose_weights(w):
            in_order = w in w_ordered
            words = (w_ordered[w] if in_order else w_raw[w])[:].bitcast(F32)
            half = (w - 1) % 2 if w > 0 else 0
            if half == 0:
                w_grouped = wg_pool.tile([P, PASSES, (2 if w > 0 else 1) * GROUP_ROWS * PACK], BF16, align_bytes=64)
                w_grouped_tiles[w] = w_grouped
            else:
                w_grouped = w_grouped_tiles[w - 1]
            cols_out = slice(half * GROUP_ROWS * PACK, (half + 1) * GROUP_ROWS * PACK)
            for g in range(PASSES):
                wt = psum.tile([P, 2, 2, P], F32, tag="bank")
                for t in range(2):
                    for u in range(2):
                        if in_order:
                            cols = slice(2 * P * g + P * u, 2 * P * g + P * (u + 1))
                        else:
                            cols = slice(2 * P * g + u, 2 * P * (g + 1), 2)
                        nc.tensor.transpose(wt[:, t, u, :], words[:, t, cols], ident[:])
                nc.scalar.copy(
                    out=w_grouped[:, g, cols_out].bitcast(F32).rearrange("p (r t u) -> p r t u", t=2, u=2),
                    in_=wt[:].rearrange("p t u r -> p r t u"),
                )
            at = group_order.index(w)
            if at + W_BUFS < GROUPS:
                load_weights(group_order[at + W_BUFS])

        def quantise_head_columns():
            nc.vector.quantize_mx(
                out=qk_codes[:].rearrange("p g r -> p (g r)").bitcast(FP8X4),
                scales=qk_scales[:].rearrange("p g r -> p (g r)"),
                in_=w_grouped_tiles[0][:].rearrange("p g r -> p (g r)"),
            )

        def quantise_block(b):
            nc.vector.quantize_mx(
                out=w_codes[:, b, :, :].rearrange("p g r -> p (g r)").bitcast(FP8X4),
                scales=w_scales[:, b, :, :].rearrange("p g r -> p (g r)"),
                in_=w_grouped_tiles[1 + 2 * b][:].rearrange("p g r -> p (g r)"),
            )

        def project(acc, m, codes, scales):
            for g in range(PASSES):
                nc.tensor.matmul_mx(
                    out=acc,
                    lhsT=h_codes[:, m, g, :].bitcast(FP8X4),
                    lhsT_scale=h_scales[:, m, g, :],
                    rhs=codes[:, g, :].bitcast(FP8X4),
                    rhs_scale=scales[:, g, :],
                    start=(g == 0),
                    stop=(g == PASSES - 1),
                )

        def q_and_k(m):
            qk = psum.tile([P, 2, QK], F32, tag="bank")
            project(qk[:].rearrange("p a c -> p (a c)"), m, qk_codes, qk_scales)
            nc.scalar.copy(out=qk_sb[:, :, m, :], in_=qk[:])

        gelu_tiles = {}

        def gate(j, m):
            pre = psum.tile([P, N_TILE], F32, tag="bank")
            project(pre[:], m, w_codes[:, UNITS + j, :, :], w_scales[:, UNITS + j, :, :])
            gelu = gelu_pool.tile([P, N_TILE], F32)
            nc.scalar.activation(out=gelu[:], in_=pre[:], func=ACT.Gelu)
            gelu_tiles[(j, m)] = gelu

        def product(j, m):
            lin = psum.tile([P, N_TILE], F32, tag="bank")
            project(lin[:], m, w_codes[:, j, :, :], w_scales[:, j, :, :])
            prod = prod_pool.tile([P, N_TILE], F32)
            nc.vector.tensor_tensor(out=prod[:], in0=lin[:], in1=gelu_tiles[(j, m)][:], op=ALU.mult)
            first = N_TILE * (j % 2)
            nc.sync.dma_start(out=g_views[j // 2][:, m, first : first + N_TILE], in_=prod[:])

        def last_cell(j, m):
            firsts = [sum(LAST_WIDTHS[:i]) for i in range(len(LAST_WIDTHS))]
            parts = []
            for first, width in zip(firsts, LAST_WIDTHS):
                cols = slice(first, first + width)
                pre = psum.tile([P, N_TILE], F32, tag="bank")
                project(pre[:, 0:width], m, w_codes[:, UNITS + j, :, cols], w_scales[:, UNITS + j, :, cols])
                gelu = gelu_pool.tile([P, N_TILE], F32)
                nc.scalar.activation(out=gelu[:, 0:width], in_=pre[:, 0:width], func=ACT.Gelu)
                parts.append(gelu)
            for first, width, gelu in zip(firsts, LAST_WIDTHS, parts):
                cols = slice(first, first + width)
                lin = psum.tile([P, N_TILE], F32, tag="bank")
                project(lin[:, 0:width], m, w_codes[:, j, :, cols], w_scales[:, j, :, cols])
                prod = prod_pool.tile([P, N_TILE], F32)
                nc.vector.tensor_tensor(out=prod[:, 0:width], in0=lin[:, 0:width], in1=gelu[:, 0:width], op=ALU.mult)
                first_out = N_TILE * (j % 2) + first
                nc.sync.dma_start(out=g_views[j // 2][:, m, first_out : first_out + width], in_=prod[:, 0:width])

        for m in range(AHEAD):
            stats_chunk(m, 0)
            stats_chunk(m, 1)
            normalise(m)
        keep_clock_up(5)
        transpose_weights(group_order[0])
        transpose_weights(group_order[1])
        keep_clock_up(1)
        transpose_tokens(0)
        stats_chunk(AHEAD, 0)
        stats_chunk(AHEAD, 1)
        quantise_block(UNITS)
        transpose_weights(group_order[2])
        keep_clock_up(1)
        quantise_tokens(0)
        transpose_weights(group_order[3])
        transpose_weights(group_order[4])
        quantise_block(0)
        normalise(AHEAD)

        rest = group_order[HEAD_GROUPS:]
        taken = 0
        for m in range(TOKEN_TILES):
            here = rest[taken : taken + STEP_GROUPS[m]]
            taken += len(here)
            if m + 1 < TOKEN_TILES:
                transpose_tokens(m + 1)
            gate(0, m)
            for i in QK_TILES[m]:
                q_and_k(i)
            if m < 2:
                scalar_stats(4, m)
            elif m in (2, 3, 4, 6):
                reorder_weights(rest[taken])
            if m + 1 + AHEAD < TOKEN_TILES:
                stats_chunk(m + 1 + AHEAD, 0)
            if m + 1 < TOKEN_TILES:
                quantise_tokens(m + 1)
            if m == 1:
                quantise_head_columns()
            if m == 6:
                quantise_block(UNITS + 1)
            if m == 7:
                quantise_block(1)
            if m + 1 + AHEAD < TOKEN_TILES:
                stats_chunk(m + 1 + AHEAD, 1)
                normalise(m + 1 + AHEAD)
            transpose_weights(here[0])
            product(0, m)
            for w in here[1:]:
                transpose_weights(w)
        nc.sync.dma_start(out=q_view, in_=qk_sb[:, 0, :, :])
        nc.sync.dma_start(out=k_view, in_=qk_sb[:, 1, :, :])

        for j in range(1, UNITS):
            for m in range(TOKEN_TILES):
                if j == UNITS - 1 and m == TOKEN_TILES - 1:
                    last_cell(j, m)
                else:
                    gate(j, m)
                    product(j, m)
                if j + 1 < UNITS and m == 0:
                    quantise_block(UNITS + j + 1)
                if j + 1 < UNITS and m == 3:
                    quantise_block(j + 1)
